import numpy as np
import ml_dtypes


def mxq(x, axis, fmt="e4m3"):
    dtype, down = {"e4m3": (ml_dtypes.float8_e4m3fn, 7), "e5m2": (ml_dtypes.float8_e5m2, 14)}[fmt]
    v = np.moveaxis(np.asarray(x, np.float32).astype(ml_dtypes.bfloat16).astype(np.float64), axis, -1)
    blocks = v.reshape(v.shape[:-1] + (-1, 32))
    amax = np.abs(blocks).max(-1, keepdims=True)
    byte = np.maximum(np.where(amax > 0, np.frexp(amax)[1] - 1 + 127, 0) - down, 1)
    scale = np.exp2(byte - 127.0)
    codes = (blocks / scale).astype(np.float32).astype(dtype).astype(np.float64)
    return np.moveaxis((codes * scale).reshape(v.shape), -1, axis)


WIDE = False


def mx_kscale(k):
    if not WIDE:
        return np.ones(k)
    levels = np.array([10, -10, 5, -5, 0])
    a = np.random.permutation(np.resize(levels, k // 512 * 4)).reshape(k // 512, 4)
    idx = np.arange(k)
    return np.exp2(a[idx // 512, idx % 128 // 32])


BF16 = ml_dtypes.bfloat16


def bf(x):
    return np.asarray(x, np.float32).astype(BF16)


def f64(x):
    return np.asarray(x).astype(np.float64)


B, C, PS, G, E = 128, 3, 64, 4, 256
NP = G * G
M1 = NP // 2
K2 = 2 * E


def setup_inputs():
    t = mx_kscale(K2)[:E]
    tt = np.concatenate([t, t])
    return {"h1": bf(np.random.standard_normal((B, NP, M1, E)) * t),
            "cross_w": bf(np.random.standard_normal((E, K2)) / np.sqrt(K2) * t[:, None] / tt[None, :]),
            "cross_b": bf(np.random.standard_normal(E) * 0.3 * t)}


def reference(h1, cross_w, cross_b):
    wq = mxq(f64(cross_w), 1, "e4m3")
    bias = f64(cross_b)
    g1 = f64(h1).reshape(B, NP, M1 // 2, K2)
    h2 = (mxq(g1, 3, "e4m3") @ wq.T) + bias
    g2 = h2.reshape(B, NP, M1 // 4, K2)
    return (mxq(g2, 3, "e4m3") @ wq.T) + bias

@@ -1,0 +1,199 @@
+from contextlib import ExitStack
+
+import concourse.mybir as mybir
+from concourse.masks import make_identity
+
+F32 = mybir.dt.float32
+BF16 = mybir.dt.bfloat16
+U32 = mybir.dt.uint32
+U8 = mybir.dt.uint8
+FP8X4 = mybir.dt.float8_e4m3fn_x4
+ADD = mybir.AluOpType.add
+IDENTITY = mybir.ActivationFunctionType.Identity
+
+P = 128
+PACK = 4
+TOKENS = 16
+FEATURES = 256
+K = 2 * FEATURES
+WORDS = K // 2
+ROWS1 = 4
+PAIRS = 2
+
+FLOPS = 2 * P * TOKENS * (ROWS1 + PAIRS) * K * FEATURES
+
+
+def tile_simplemodel_pc_t_kernel(tc, h1, cross_w, cross_b, out):
+    nc = tc.nc
+    h1_rows = h1.rearrange("b i (m n) f -> b i m (n f)", n=2)
+    out_rows = out.rearrange("b i m f -> b i (m f)")
+
+    with ExitStack() as ctx:
+        ctx.enter_context(tc.manual_schedule())
+        keep = ctx.enter_context(tc.tile_pool(name="keep", bufs=1))
+        ring = ctx.enter_context(tc.tile_pool(name="ring", bufs=3))
+        psum_t = ctx.enter_context(tc.psum_pool(name="psum_t", bufs=4))
+        psum_1 = ctx.enter_context(tc.psum_pool(name="psum_1", bufs=2))
+        psum_2 = ctx.enter_context(tc.psum_pool(name="psum_2", bufs=2))
+
+        w_rows = keep.tile([P, 2, K], BF16)
+        nc.sync.dma_start(out=w_rows[:], in_=cross_w.rearrange("(q e) k -> q e k", e=2))
+        x_all = keep.tile([P, TOKENS, ROWS1, K], BF16)
+        for token in range(TOKENS):
+            nc.sync.dma_start(out=x_all[:, token], in_=h1_rows[:, token])
+        out_all = keep.tile([P, TOKENS, PAIRS, FEATURES], F32)
+
+        ident = keep.tile([P, P], F32)
+        make_identity(nc, ident[:])
+        ones = keep.tile([P, P], BF16)
+        nc.vector.memset(ones[:], 1.0)
+        bias_row = keep.tile([P, FEATURES], BF16)
+        nc.vector.memset(bias_row[:], 0.0)
+        nc.scalar.dma_start(out=bias_row[0:1, :], in_=cross_b.unsqueeze(0))
+
+        def transpose_two_rows(words, bank):
+            for r in range(2):
+                for u in range(2):
+                    nc.tensor.transpose(bank[:, r, u, :], words[:, r, u * P : (u + 1) * P], ident[:])
+
+        def regroup_two_rows(bank, grouped_words):
+            nc.scalar.copy(out=grouped_words, in_=bank[:].rearrange("q r u c -> q r c u"))
+
+        bias_bank = psum_2.tile([P, FEATURES], F32, tag="level2")
+        nc.tensor.matmul(out=bias_bank[:], lhsT=ones[:], rhs=bias_row[:], start=True, stop=True)
+        bias_free = keep.tile([P, FEATURES], F32)
+        nc.vector.tensor_copy(out=bias_free[:], in_=bias_bank[:])
+
+        w_bank = psum_t.tile([P, 2, 2, P], F32, tag="transposed")
+        transpose_two_rows(w_rows[:].bitcast(F32), w_bank)
+        w_grouped = keep.tile([P, 2, P, PACK], BF16, align_bytes=64)
+        regroup_two_rows(w_bank, w_grouped[:].bitcast(F32))
+        w_codes = keep.tile([P, 2, P], U32, align_bytes=64)
+        w_scales = keep.tile([P, 2, P], U8, align_bytes=64)
+        nc.vector.quantize_mx(
+            out=w_codes[:].rearrange("p e q -> p (e q)").bitcast(FP8X4),
+            scales=w_scales[:].rearrange("p e q -> p (e q)"),
+            in_=w_grouped[:].rearrange("p e q t -> p (e q t)"),
+        )
+
+        bias_t = psum_t.tile([P, 2, P], F32, tag="transposed")
+        for e in range(2):
+            nc.tensor.transpose(
+                bias_t[:, e, :], bias_free[:].rearrange("p (q e) -> p e q", e=2)[:, e, :], ident[:]
+            )
+        bias_part = keep.tile([P, 2], F32)
+        nc.vector.tensor_copy(out=bias_part[:], in_=bias_t[:, :, 0])
+
+        t_banks = {}
+        grouped1 = {}
+        codes1 = {}
+        banks1 = {}
+        grouped2 = {}
+        codes2 = {}
+        banks2 = {}
+
+        def transposes(token):
+            t_banks[token] = []
+            for j in range(PAIRS):
+                t_bank = psum_t.tile([P, 2, 2, P], F32, tag="transposed")
+                transpose_two_rows(x_all[:, token, 2 * j : 2 * j + 2, :].bitcast(F32), t_bank)
+                t_banks[token].append(t_bank)
+
+        def regroup1(token):
+            g1_grouped = ring.tile([P, ROWS1, P, PACK], BF16, align_bytes=64)
+            for j in range(PAIRS):
+                regroup_two_rows(t_banks[token][j], g1_grouped[:, 2 * j : 2 * j + 2].bitcast(F32))
+            grouped1[token] = g1_grouped
+
+        def quantise1(token):
+            g1_codes = ring.tile([P, ROWS1 * P], U32, align_bytes=64)
+            g1_scales = ring.tile([P, ROWS1 * P], U8, align_bytes=64)
+            nc.vector.quantize_mx(
+                out=g1_codes[:].bitcast(FP8X4),
+                scales=g1_scales[:],
+                in_=grouped1[token][:].rearrange("p m b t -> p (m b t)"),
+            )
+            codes1[token] = (g1_codes, g1_scales)
+
+        def level1(token):
+            g1_codes, g1_scales = codes1[token]
+            banks1[token] = []
+            for j in range(PAIRS):
+                h2_bank = psum_1.tile([P, 2, 2 * P], F32)
+                cols = slice(j * 2 * P, (j + 1) * 2 * P)
+                for e in range(2):
+                    nc.tensor.matmul_mx(
+                        out=h2_bank[:, e, :],
+                        lhsT=w_codes[:, e, :].bitcast(FP8X4),
+                        lhsT_scale=w_scales[:, e, :],
+                        rhs=g1_codes[:, cols].bitcast(FP8X4),
+                        rhs_scale=g1_scales[:, cols],
+                        start=True,
+                        stop=True,
+                    )
+                banks1[token].append(h2_bank)
+
+        def regroup2(token):
+            g2_grouped = ring.tile([P, PAIRS, P, 2, 2], BF16, align_bytes=64)
+            nc.vector.tensor_tensor(
+                out=g2_grouped[:, 0],
+                in0=banks1[token][0][:].rearrange("q e (u b) -> q b u e", u=2),
+                in1=bias_part[:].unsqueeze(1).unsqueeze(1).to_broadcast([P, P, 2, 2]),
+                op=ADD,
+            )
+            for e in range(2):
+                nc.scalar.activation(
+                    out=g2_grouped[:, 1, :, :, e],
+                    in_=banks1[token][1][:, e, :].rearrange("q (u b) -> q b u", u=2),
+                    func=IDENTITY,
+                    bias=bias_part[:, e : e + 1],
+                )
+            grouped2[token] = g2_grouped
+
+        def quantise2(token):
+            g2_codes = ring.tile([P, PAIRS * P], U32, align_bytes=64)
+            g2_scales = ring.tile([P, PAIRS * P], U8, align_bytes=64)
+            nc.vector.quantize_mx(
+                out=g2_codes[:].bitcast(FP8X4),
+                scales=g2_scales[:],
+                in_=grouped2[token][:].rearrange("p j b u e -> p (j b u e)"),
+            )
+            codes2[token] = (g2_codes, g2_scales)
+
+        def level2(token):
+            g2_codes, g2_scales = codes2[token]
+            out_bank = psum_2.tile([P, PAIRS, FEATURES], F32, tag="level2")
+            for j in range(PAIRS):
+                nc.tensor.matmul_mx(
+                    out=out_bank[:, j, :],
+                    lhsT=g2_codes[:, j * P : (j + 1) * P].bitcast(FP8X4),
+                    lhsT_scale=g2_scales[:, j * P : (j + 1) * P],
+                    rhs=w_codes[:].rearrange("p e q -> p (e q)").bitcast(FP8X4),
+                    rhs_scale=w_scales[:].rearrange("p e q -> p (e q)"),
+                    start=True,
+                    stop=True,
+                )
+            banks2[token] = out_bank
+
+        def finish(token):
+            nc.vector.tensor_tensor(
+                out=out_all[:, token].rearrange("b j (q e) -> b j q e", e=2),
+                in0=banks2[token][:].rearrange("b j (e q) -> b j q e", e=2),
+                in1=bias_free[:].rearrange("b (q e) -> b q e", e=2).unsqueeze(1).to_broadcast([P, PAIRS, P, 2]),
+                op=ADD,
+            )
+            nc.sync.dma_start(out=out_rows[:, token], in_=out_all[:, token].rearrange("b j f -> b (j f)"))
+
+        def run(stage, token):
+            if 0 <= token < TOKENS:
+                stage(token)
+
+        for step in range(-2, TOKENS + 2):
+            run(quantise1, step)
+            run(level2, step - 2)
+            run(finish, step - 2)
+            run(level1, step)
+            run(regroup1, step + 1)
+            run(regroup2, step)
+            run(quantise2, step - 1)
+            run(transposes, step + 2)

@@ -33,11 +33,14 @@ def tile_simplemodel_pc_t_kernel(tc, h1, cross_w, cross_b, out):
         keep = ctx.enter_context(tc.tile_pool(name="keep", bufs=1))
         ring = ctx.enter_context(tc.tile_pool(name="ring", bufs=3))
         psum_t = ctx.enter_context(tc.psum_pool(name="psum_t", bufs=4))
-        psum_1 = ctx.enter_context(tc.psum_pool(name="psum_1", bufs=2))
-        psum_2 = ctx.enter_context(tc.psum_pool(name="psum_2", bufs=2))
+        psum_1 = ctx.enter_context(tc.psum_pool(name="psum_1", bufs=3))
+        psum_2 = ctx.enter_context(tc.psum_pool(name="psum_2", bufs=1))
 
         w_rows = keep.tile([P, 2, K], BF16)
         nc.sync.dma_start(out=w_rows[:], in_=cross_w.rearrange("(q e) k -> q e k", e=2))
+        bias_row = keep.tile([P, FEATURES], BF16)
+        nc.vector.memset(bias_row[:], 0.0)
+        nc.sync.dma_start(out=bias_row[0:1, :], in_=cross_b.unsqueeze(0))
         x_all = keep.tile([P, TOKENS, ROWS1, K], BF16)
         for token in range(TOKENS):
             nc.sync.dma_start(out=x_all[:, token], in_=h1_rows[:, token])
@@ -47,9 +50,6 @@ def tile_simplemodel_pc_t_kernel(tc, h1, cross_w, cross_b, out):
         make_identity(nc, ident[:])
         ones = keep.tile([P, P], BF16)
         nc.vector.memset(ones[:], 1.0)
-        bias_row = keep.tile([P, FEATURES], BF16)
-        nc.vector.memset(bias_row[:], 0.0)
-        nc.scalar.dma_start(out=bias_row[0:1, :], in_=cross_b.unsqueeze(0))
 
         def transpose_two_rows(words, bank):
             for r in range(2):
@@ -59,13 +59,22 @@ def tile_simplemodel_pc_t_kernel(tc, h1, cross_w, cross_b, out):
         def regroup_two_rows(bank, grouped_words):
             nc.scalar.copy(out=grouped_words, in_=bank[:].rearrange("q r u c -> q r c u"))
 
+        w_bank = psum_t.tile([P, 2, 2, P], F32, tag="transposed")
+        transpose_two_rows(w_rows[:].bitcast(F32), w_bank)
+
         bias_bank = psum_2.tile([P, FEATURES], F32, tag="level2")
         nc.tensor.matmul(out=bias_bank[:], lhsT=ones[:], rhs=bias_row[:], start=True, stop=True)
         bias_free = keep.tile([P, FEATURES], F32)
         nc.vector.tensor_copy(out=bias_free[:], in_=bias_bank[:])
 
-        w_bank = psum_t.tile([P, 2, 2, P], F32, tag="transposed")
-        transpose_two_rows(w_rows[:].bitcast(F32), w_bank)
+        bias_t = psum_t.tile([P, 2, P], F32, tag="transposed")
+        for e in range(2):
+            nc.tensor.transpose(
+                bias_t[:, e, :], bias_free[:].rearrange("p (q e) -> p e q", e=2)[:, e, :], ident[:]
+            )
+        bias_part = keep.tile([P, 2], F32)
+        nc.vector.tensor_copy(out=bias_part[:], in_=bias_t[:, :, 0])
+
         w_grouped = keep.tile([P, 2, P, PACK], BF16, align_bytes=64)
         regroup_two_rows(w_bank, w_grouped[:].bitcast(F32))
         w_codes = keep.tile([P, 2, P], U32, align_bytes=64)
@@ -75,14 +84,6 @@ def tile_simplemodel_pc_t_kernel(tc, h1, cross_w, cross_b, out):
             scales=w_scales[:].rearrange("p e q -> p (e q)"),
             in_=w_grouped[:].rearrange("p e q t -> p (e q t)"),
         )
-
-        bias_t = psum_t.tile([P, 2, P], F32, tag="transposed")
-        for e in range(2):
-            nc.tensor.transpose(
-                bias_t[:, e, :], bias_free[:].rearrange("p (q e) -> p e q", e=2)[:, e, :], ident[:]
-            )
-        bias_part = keep.tile([P, 2], F32)
-        nc.vector.tensor_copy(out=bias_part[:], in_=bias_t[:, :, 0])
 
         t_banks = {}
         grouped1 = {}
@@ -188,12 +189,12 @@ def tile_simplemodel_pc_t_kernel(tc, h1, cross_w, cross_b, out):
             if 0 <= token < TOKENS:
                 stage(token)
 
-        for step in range(-2, TOKENS + 2):
+        for step in range(-2, TOKENS + 3):
             run(quantise1, step)
-            run(level2, step - 2)
-            run(finish, step - 2)
+            run(finish, step - 3)
             run(level1, step)
+            run(level2, step - 2)
+            run(quantise2, step - 1)
             run(regroup1, step + 1)
             run(regroup2, step)
-            run(quantise2, step - 1)
             run(transposes, step + 2)

@@ -33,16 +33,17 @@ def tile_simplemodel_pc_t_kernel(tc, h1, cross_w, cross_b, out):
         keep = ctx.enter_context(tc.tile_pool(name="keep", bufs=1))
         ring = ctx.enter_context(tc.tile_pool(name="ring", bufs=3))
         psum_t = ctx.enter_context(tc.psum_pool(name="psum_t", bufs=4))
-        psum_1 = ctx.enter_context(tc.psum_pool(name="psum_1", bufs=3))
-        psum_2 = ctx.enter_context(tc.psum_pool(name="psum_2", bufs=1))
+        psum_1 = ctx.enter_context(tc.psum_pool(name="psum_1", bufs=2))
+        psum_2 = ctx.enter_context(tc.psum_pool(name="psum_2", bufs=2))
 
+        x_all = keep.tile([P, TOKENS, ROWS1, K], BF16)
+        nc.sync.dma_start(out=x_all[:, 0], in_=h1_rows[:, 0])
         w_rows = keep.tile([P, 2, K], BF16)
         nc.sync.dma_start(out=w_rows[:], in_=cross_w.rearrange("(q e) k -> q e k", e=2))
         bias_row = keep.tile([P, FEATURES], BF16)
         nc.vector.memset(bias_row[:], 0.0)
         nc.sync.dma_start(out=bias_row[0:1, :], in_=cross_b.unsqueeze(0))
-        x_all = keep.tile([P, TOKENS, ROWS1, K], BF16)
-        for token in range(TOKENS):
+        for token in range(1, TOKENS):
             nc.sync.dma_start(out=x_all[:, token], in_=h1_rows[:, token])
         out_all = keep.tile([P, TOKENS, PAIRS, FEATURES], F32)
 
@@ -56,34 +57,8 @@ def tile_simplemodel_pc_t_kernel(tc, h1, cross_w, cross_b, out):
                 for u in range(2):
                     nc.tensor.transpose(bank[:, r, u, :], words[:, r, u * P : (u + 1) * P], ident[:])
 
-        def regroup_two_rows(bank, grouped_words):
-            nc.scalar.copy(out=grouped_words, in_=bank[:].rearrange("q r u c -> q r c u"))
-
-        w_bank = psum_t.tile([P, 2, 2, P], F32, tag="transposed")
-        transpose_two_rows(w_rows[:].bitcast(F32), w_bank)
-
-        bias_bank = psum_2.tile([P, FEATURES], F32, tag="level2")
-        nc.tensor.matmul(out=bias_bank[:], lhsT=ones[:], rhs=bias_row[:], start=True, stop=True)
-        bias_free = keep.tile([P, FEATURES], F32)
-        nc.vector.tensor_copy(out=bias_free[:], in_=bias_bank[:])
-
-        bias_t = psum_t.tile([P, 2, P], F32, tag="transposed")
-        for e in range(2):
-            nc.tensor.transpose(
-                bias_t[:, e, :], bias_free[:].rearrange("p (q e) -> p e q", e=2)[:, e, :], ident[:]
-            )
-        bias_part = keep.tile([P, 2], F32)
-        nc.vector.tensor_copy(out=bias_part[:], in_=bias_t[:, :, 0])
-
-        w_grouped = keep.tile([P, 2, P, PACK], BF16, align_bytes=64)
-        regroup_two_rows(w_bank, w_grouped[:].bitcast(F32))
-        w_codes = keep.tile([P, 2, P], U32, align_bytes=64)
-        w_scales = keep.tile([P, 2, P], U8, align_bytes=64)
-        nc.vector.quantize_mx(
-            out=w_codes[:].rearrange("p e q -> p (e q)").bitcast(FP8X4),
-            scales=w_scales[:].rearrange("p e q -> p (e q)"),
-            in_=w_grouped[:].rearrange("p e q t -> p (e q t)"),
-        )
+        def regroup_two_rows(copy, bank, grouped_words):
+            copy(out=grouped_words, in_=bank[:].rearrange("q r u c -> q r c u"))
 
         t_banks = {}
         grouped1 = {}
@@ -103,7 +78,7 @@ def tile_simplemodel_pc_t_kernel(tc, h1, cross_w, cross_b, out):
         def regroup1(token):
             g1_grouped = ring.tile([P, ROWS1, P, PACK], BF16, align_bytes=64)
             for j in range(PAIRS):
-                regroup_two_rows(t_banks[token][j], g1_grouped[:, 2 * j : 2 * j + 2].bitcast(F32))
+                regroup_two_rows(nc.scalar.copy, t_banks[token][j], g1_grouped[:, 2 * j : 2 * j + 2].bitcast(F32))
             grouped1[token] = g1_grouped
 
         def quantise1(token):
@@ -185,11 +160,39 @@ def tile_simplemodel_pc_t_kernel(tc, h1, cross_w, cross_b, out):
             )
             nc.sync.dma_start(out=out_rows[:, token], in_=out_all[:, token].rearrange("b j f -> b (j f)"))
 
+        transposes(0)
+
+        w_bank = psum_t.tile([P, 2, 2, P], F32, tag="transposed")
+        transpose_two_rows(w_rows[:].bitcast(F32), w_bank)
+
+        bias_bank = psum_2.tile([P, FEATURES], F32, tag="level2")
+        nc.tensor.matmul(out=bias_bank[:], lhsT=ones[:], rhs=bias_row[:], start=True, stop=True)
+        bias_free = keep.tile([P, FEATURES], F32)
+        nc.vector.tensor_copy(out=bias_free[:], in_=bias_bank[:])
+
+        bias_t = psum_t.tile([P, 2, P], F32, tag="transposed")
+        for e in range(2):
+            nc.tensor.transpose(
+                bias_t[:, e, :], bias_free[:].rearrange("p (q e) -> p e q", e=2)[:, e, :], ident[:]
+            )
+        bias_part = keep.tile([P, 2], F32)
+        nc.vector.tensor_copy(out=bias_part[:], in_=bias_t[:, :, 0])
+
+        w_grouped = keep.tile([P, 2, P, PACK], BF16, align_bytes=64)
+        regroup_two_rows(nc.vector.tensor_copy, w_bank, w_grouped[:].bitcast(F32))
+        w_codes = keep.tile([P, 2, P], U32, align_bytes=64)
+        w_scales = keep.tile([P, 2, P], U8, align_bytes=64)
+        nc.vector.quantize_mx(
+            out=w_codes[:].rearrange("p e q -> p (e q)").bitcast(FP8X4),
+            scales=w_scales[:].rearrange("p e q -> p (e q)"),
+            in_=w_grouped[:].rearrange("p e q t -> p (e q t)"),
+        )
+
         def run(stage, token):
             if 0 <= token < TOKENS:
                 stage(token)
 
-        for step in range(-2, TOKENS + 3):
+        for step in range(-1, TOKENS + 3):
             run(quantise1, step)
             run(finish, step - 3)
             run(level1, step)

@@ -32,8 +32,8 @@ def tile_simplemodel_pc_t_kernel(tc, h1, cross_w, cross_b, out):
         ctx.enter_context(tc.manual_schedule())
         keep = ctx.enter_context(tc.tile_pool(name="keep", bufs=1))
         ring = ctx.enter_context(tc.tile_pool(name="ring", bufs=3))
-        psum_t = ctx.enter_context(tc.psum_pool(name="psum_t", bufs=4))
-        psum_1 = ctx.enter_context(tc.psum_pool(name="psum_1", bufs=2))
+        psum_t = ctx.enter_context(tc.psum_pool(name="psum_t", bufs=3))
+        psum_1 = ctx.enter_context(tc.psum_pool(name="psum_1", bufs=3))
         psum_2 = ctx.enter_context(tc.psum_pool(name="psum_2", bufs=2))
 
         x_all = keep.tile([P, TOKENS, ROWS1, K], BF16)
@@ -95,7 +95,7 @@ def tile_simplemodel_pc_t_kernel(tc, h1, cross_w, cross_b, out):
             g1_codes, g1_scales = codes1[token]
             banks1[token] = []
             for j in range(PAIRS):
-                h2_bank = psum_1.tile([P, 2, 2 * P], F32)
+                h2_bank = psum_1.tile([P, 2, 2 * P], F32, tag="level1")
                 cols = slice(j * 2 * P, (j + 1) * 2 * P)
                 for e in range(2):
                     nc.tensor.matmul_mx(
@@ -162,7 +162,7 @@ def tile_simplemodel_pc_t_kernel(tc, h1, cross_w, cross_b, out):
 
         transposes(0)
 
-        w_bank = psum_t.tile([P, 2, 2, P], F32, tag="transposed")
+        w_bank = psum_1.tile([P, 2, 2, P], F32, tag="level1")
         transpose_two_rows(w_rows[:].bitcast(F32), w_bank)
 
         bias_bank = psum_2.tile([P, FEATURES], F32, tag="level2")
@@ -170,7 +170,7 @@ def tile_simplemodel_pc_t_kernel(tc, h1, cross_w, cross_b, out):
         bias_free = keep.tile([P, FEATURES], F32)
         nc.vector.tensor_copy(out=bias_free[:], in_=bias_bank[:])
 
-        bias_t = psum_t.tile([P, 2, P], F32, tag="transposed")
+        bias_t = psum_1.tile([P, 2, P], F32, tag="level1")
         for e in range(2):
             nc.tensor.transpose(
                 bias_t[:, e, :], bias_free[:].rearrange("p (q e) -> p e q", e=2)[:, e, :], ident[:]
@@ -192,12 +192,12 @@ def tile_simplemodel_pc_t_kernel(tc, h1, cross_w, cross_b, out):
             if 0 <= token < TOKENS:
                 stage(token)
 
-        for step in range(-1, TOKENS + 3):
+        for step in range(-1, TOKENS + 4):
             run(quantise1, step)
-            run(finish, step - 3)
-            run(level1, step)
-            run(level2, step - 2)
-            run(quantise2, step - 1)
+            run(finish, step - 4)
+            run(level1, step - 1)
+            run(level2, step - 3)
+            run(quantise2, step - 2)
             run(regroup1, step + 1)
-            run(regroup2, step)
+            run(regroup2, step - 1)
             run(transposes, step + 2)

@@ -18,6 +18,7 @@ FEATURES = 256
 K = 2 * FEATURES
 WORDS = K // 2
 ROWS1 = 4
+SHARED_TOKENS = 4
 PAIRS = 2
 
 FLOPS = 2 * P * TOKENS * (ROWS1 + PAIRS) * K * FEATURES
@@ -37,14 +38,24 @@ def tile_simplemodel_pc_t_kernel(tc, h1, cross_w, cross_b, out):
         psum_2 = ctx.enter_context(tc.psum_pool(name="psum_2", bufs=2))
 
         x_all = keep.tile([P, TOKENS, ROWS1, K], BF16)
-        nc.sync.dma_start(out=x_all[:, 0], in_=h1_rows[:, 0])
+
+        def load_pair(token, j):
+            rows = slice(2 * j, 2 * j + 2)
+            nc.sync.dma_start(out=x_all[:, token, rows], in_=h1_rows[:, token, rows])
+
+        load_pair(0, 0)
+        load_pair(0, 1)
         w_rows = keep.tile([P, 2, K], BF16)
         nc.sync.dma_start(out=w_rows[:], in_=cross_w.rearrange("(q e) k -> q e k", e=2))
+        load_pair(1, 0)
+        load_pair(1, 1)
+        for token in range(2, TOKENS):
+            nc.sync.dma_start(out=x_all[:, token], in_=h1_rows[:, token])
+        bias_pair = keep.tile([P, 2], BF16)
+        nc.scalar.dma_start(out=bias_pair[:], in_=cross_b.rearrange("(q e) -> q e", e=2))
         bias_row = keep.tile([P, FEATURES], BF16)
         nc.vector.memset(bias_row[:], 0.0)
-        nc.sync.dma_start(out=bias_row[0:1, :], in_=cross_b.unsqueeze(0))
-        for token in range(1, TOKENS):
-            nc.sync.dma_start(out=x_all[:, token], in_=h1_rows[:, token])
+        nc.scalar.dma_start(out=bias_row[0:1, :], in_=cross_b.unsqueeze(0))
         out_all = keep.tile([P, TOKENS, PAIRS, FEATURES], F32)
 
         ident = keep.tile([P, P], F32)
@@ -77,8 +88,9 @@ def tile_simplemodel_pc_t_kernel(tc, h1, cross_w, cross_b, out):
 
         def regroup1(token):
             g1_grouped = ring.tile([P, ROWS1, P, PACK], BF16, align_bytes=64)
-            for j in range(PAIRS):
-                regroup_two_rows(nc.scalar.copy, t_banks[token][j], g1_grouped[:, 2 * j : 2 * j + 2].bitcast(F32))
+            second = nc.vector.tensor_copy if token < SHARED_TOKENS else nc.scalar.copy
+            for j, copy in enumerate((nc.scalar.copy, second)):
+                regroup_two_rows(copy, t_banks[token][j], g1_grouped[:, 2 * j : 2 * j + 2].bitcast(F32))
             grouped1[token] = g1_grouped
 
         def quantise1(token):
@@ -161,25 +173,20 @@ def tile_simplemodel_pc_t_kernel(tc, h1, cross_w, cross_b, out):
             nc.sync.dma_start(out=out_rows[:, token], in_=out_all[:, token].rearrange("b j f -> b (j f)"))
 
         transposes(0)
-
         w_bank = psum_1.tile([P, 2, 2, P], F32, tag="level1")
         transpose_two_rows(w_rows[:].bitcast(F32), w_bank)
-
         bias_bank = psum_2.tile([P, FEATURES], F32, tag="level2")
         nc.tensor.matmul(out=bias_bank[:], lhsT=ones[:], rhs=bias_row[:], start=True, stop=True)
-        bias_free = keep.tile([P, FEATURES], F32)
-        nc.vector.tensor_copy(out=bias_free[:], in_=bias_bank[:])
+        transposes(1)
 
-        bias_t = psum_1.tile([P, 2, P], F32, tag="level1")
-        for e in range(2):
-            nc.tensor.transpose(
-                bias_t[:, e, :], bias_free[:].rearrange("p (q e) -> p e q", e=2)[:, e, :], ident[:]
-            )
         bias_part = keep.tile([P, 2], F32)
-        nc.vector.tensor_copy(out=bias_part[:], in_=bias_t[:, :, 0])
-
+        nc.vector.tensor_copy(out=bias_part[:], in_=bias_pair[:])
+        regroup1(0)
         w_grouped = keep.tile([P, 2, P, PACK], BF16, align_bytes=64)
-        regroup_two_rows(nc.vector.tensor_copy, w_bank, w_grouped[:].bitcast(F32))
+        regroup_two_rows(nc.scalar.copy, w_bank, w_grouped[:].bitcast(F32))
+        bias_free = keep.tile([P, FEATURES], F32)
+        nc.scalar.copy(out=bias_free[:], in_=bias_bank[:])
+        quantise1(0)
         w_codes = keep.tile([P, 2, P], U32, align_bytes=64)
         w_scales = keep.tile([P, 2, P], U8, align_bytes=64)
         nc.vector.quantize_mx(
@@ -192,12 +199,13 @@ def tile_simplemodel_pc_t_kernel(tc, h1, cross_w, cross_b, out):
             if 0 <= token < TOKENS:
                 stage(token)
 
-        for step in range(-1, TOKENS + 4):
-            run(quantise1, step)
-            run(finish, step - 4)
+        for step in range(TOKENS + 3):
+            if step > 0:
+                run(quantise1, step)
             run(level1, step - 1)
             run(level2, step - 3)
-            run(quantise2, step - 2)
             run(regroup1, step + 1)
             run(regroup2, step - 1)
+            run(quantise2, step - 2)
+            run(finish, step - 3)
             run(transposes, step + 2)

@@ -123,19 +123,23 @@ def tile_simplemodel_pc_t_kernel(tc, h1, cross_w, cross_b, out):
 
         def regroup2(token):
             g2_grouped = ring.tile([P, PAIRS, P, 2, 2], BF16, align_bytes=64)
-            nc.vector.tensor_tensor(
-                out=g2_grouped[:, 0],
-                in0=banks1[token][0][:].rearrange("q e (u b) -> q b u e", u=2),
-                in1=bias_part[:].unsqueeze(1).unsqueeze(1).to_broadcast([P, P, 2, 2]),
-                op=ADD,
-            )
-            for e in range(2):
-                nc.scalar.activation(
-                    out=g2_grouped[:, 1, :, :, e],
-                    in_=banks1[token][1][:, e, :].rearrange("q (u b) -> q b u", u=2),
-                    func=IDENTITY,
-                    bias=bias_part[:, e : e + 1],
-                )
+            scalar_pairs = () if token % 2 == 0 else (0, 1)
+            for j in range(PAIRS):
+                if j in scalar_pairs:
+                    for e in range(2):
+                        nc.scalar.activation(
+                            out=g2_grouped[:, j, :, :, e],
+                            in_=banks1[token][j][:, e, :].rearrange("q (u b) -> q b u", u=2),
+                            func=IDENTITY,
+                            bias=bias_part[:, e : e + 1],
+                        )
+                else:
+                    nc.vector.tensor_tensor(
+                        out=g2_grouped[:, j],
+                        in0=banks1[token][j][:].rearrange("q e (u b) -> q b u e", u=2),
+                        in1=bias_part[:].unsqueeze(1).unsqueeze(1).to_broadcast([P, P, 2, 2]),
+                        op=ADD,
+                    )
             grouped2[token] = g2_grouped
 
         def quantise2(token):

@@ -19,6 +19,8 @@ K = 2 * FEATURES
 WORDS = K // 2
 ROWS1 = 4
 SHARED_TOKENS = 4
+WARM_MATMULS = 3
+WARM_COLS = 512
 PAIRS = 2
 
 FLOPS = 2 * P * TOKENS * (ROWS1 + PAIRS) * K * FEATURES
@@ -27,7 +29,6 @@ FLOPS = 2 * P * TOKENS * (ROWS1 + PAIRS) * K * FEATURES
 def tile_simplemodel_pc_t_kernel(tc, h1, cross_w, cross_b, out):
     nc = tc.nc
     h1_rows = h1.rearrange("b i (m n) f -> b i m (n f)", n=2)
-    out_rows = out.rearrange("b i m f -> b i (m f)")
 
     with ExitStack() as ctx:
         ctx.enter_context(tc.manual_schedule())
@@ -37,6 +38,8 @@ def tile_simplemodel_pc_t_kernel(tc, h1, cross_w, cross_b, out):
         psum_1 = ctx.enter_context(tc.psum_pool(name="psum_1", bufs=3))
         psum_2 = ctx.enter_context(tc.psum_pool(name="psum_2", bufs=2))
 
+        ones = keep.tile([P, WARM_COLS], BF16)
+        nc.vector.memset(ones[:], 1.0)
         x_all = keep.tile([P, TOKENS, ROWS1, K], BF16)
 
         def load_pair(token, j):
@@ -60,8 +63,6 @@ def tile_simplemodel_pc_t_kernel(tc, h1, cross_w, cross_b, out):
 
         ident = keep.tile([P, P], F32)
         make_identity(nc, ident[:])
-        ones = keep.tile([P, P], BF16)
-        nc.vector.memset(ones[:], 1.0)
 
         def transpose_two_rows(words, bank):
             for r in range(2):
@@ -103,37 +104,48 @@ def tile_simplemodel_pc_t_kernel(tc, h1, cross_w, cross_b, out):
             )
             codes1[token] = (g1_codes, g1_scales)
 
+        def on_scalar(token):
+            return token % 2 == 1
+
         def level1(token):
             g1_codes, g1_scales = codes1[token]
             banks1[token] = []
-            for j in range(PAIRS):
-                h2_bank = psum_1.tile([P, 2, 2 * P], F32, tag="level1")
-                cols = slice(j * 2 * P, (j + 1) * 2 * P)
+
+            def one_pass(product, e, cols):
+                nc.tensor.matmul_mx(
+                    out=product,
+                    lhsT=w_codes[:, e, :].bitcast(FP8X4),
+                    lhsT_scale=w_scales[:, e, :],
+                    rhs=g1_codes[:, cols].bitcast(FP8X4),
+                    rhs_scale=g1_scales[:, cols],
+                    start=True,
+                    stop=True,
+                )
+
+            if on_scalar(token):
                 for e in range(2):
-                    nc.tensor.matmul_mx(
-                        out=h2_bank[:, e, :],
-                        lhsT=w_codes[:, e, :].bitcast(FP8X4),
-                        lhsT_scale=w_scales[:, e, :],
-                        rhs=g1_codes[:, cols].bitcast(FP8X4),
-                        rhs_scale=g1_scales[:, cols],
-                        start=True,
-                        stop=True,
-                    )
-                banks1[token].append(h2_bank)
+                    h2_bank = psum_1.tile([P, ROWS1 * P], F32, tag="level1")
+                    one_pass(h2_bank[:], e, slice(0, ROWS1 * P))
+                    banks1[token].append(h2_bank)
+            else:
+                for j in range(PAIRS):
+                    h2_bank = psum_1.tile([P, 2, 2 * P], F32, tag="level1")
+                    for e in range(2):
+                        one_pass(h2_bank[:, e, :], e, slice(j * 2 * P, (j + 1) * 2 * P))
+                    banks1[token].append(h2_bank)
 
         def regroup2(token):
             g2_grouped = ring.tile([P, PAIRS, P, 2, 2], BF16, align_bytes=64)
-            scalar_pairs = () if token % 2 == 0 else (0, 1)
-            for j in range(PAIRS):
-                if j in scalar_pairs:
-                    for e in range(2):
-                        nc.scalar.activation(
-                            out=g2_grouped[:, j, :, :, e],
-                            in_=banks1[token][j][:, e, :].rearrange("q (u b) -> q b u", u=2),
-                            func=IDENTITY,
-                            bias=bias_part[:, e : e + 1],
-                        )
-                else:
+            if on_scalar(token):
+                for e in range(2):
+                    nc.scalar.activation(
+                        out=g2_grouped[:, :, :, :, e],
+                        in_=banks1[token][e][:].rearrange("q (j u b) -> q j b u", j=PAIRS, u=2),
+                        func=IDENTITY,
+                        bias=bias_part[:, e : e + 1],
+                    )
+            else:
+                for j in range(PAIRS):
                     nc.vector.tensor_tensor(
                         out=g2_grouped[:, j],
                         in0=banks1[token][j][:].rearrange("q e (u b) -> q b u e", u=2),
@@ -168,19 +180,23 @@ def tile_simplemodel_pc_t_kernel(tc, h1, cross_w, cross_b, out):
             banks2[token] = out_bank
 
         def finish(token):
-            nc.vector.tensor_tensor(
-                out=out_all[:, token].rearrange("b j (q e) -> b j q e", e=2),
-                in0=banks2[token][:].rearrange("b j (e q) -> b j q e", e=2),
-                in1=bias_free[:].rearrange("b (q e) -> b q e", e=2).unsqueeze(1).to_broadcast([P, PAIRS, P, 2]),
-                op=ADD,
-            )
-            nc.sync.dma_start(out=out_rows[:, token], in_=out_all[:, token].rearrange("b j f -> b (j f)"))
+            parts = [slice(0, PAIRS)] if token < TOKENS - 1 else [slice(j, j + 1) for j in range(PAIRS)]
+            for part in parts:
+                pairs = part.stop - part.start
+                nc.vector.tensor_tensor(
+                    out=out_all[:, token, part].rearrange("b j (q e) -> b j q e", e=2),
+                    in0=banks2[token][:, part].rearrange("b j (e q) -> b j q e", e=2),
+                    in1=bias_free[:].rearrange("b (q e) -> b q e", e=2).unsqueeze(1).to_broadcast([P, pairs, P, 2]),
+                    op=ADD,
+                )
+                nc.sync.dma_start(out=out[:, token, part], in_=out_all[:, token, part])
 
+        warm_bank = psum_2.tile([P, WARM_COLS], F32, tag="level2")
+        for i in range(WARM_MATMULS):
+            nc.tensor.matmul(out=warm_bank[:], lhsT=ones[:, :P], rhs=ones[:], start=True, stop=True)
         transposes(0)
         w_bank = psum_1.tile([P, 2, 2, P], F32, tag="level1")
         transpose_two_rows(w_rows[:].bitcast(F32), w_bank)
-        bias_bank = psum_2.tile([P, FEATURES], F32, tag="level2")
-        nc.tensor.matmul(out=bias_bank[:], lhsT=ones[:], rhs=bias_row[:], start=True, stop=True)
         transposes(1)
 
         bias_part = keep.tile([P, 2], F32)
@@ -188,8 +204,6 @@ def tile_simplemodel_pc_t_kernel(tc, h1, cross_w, cross_b, out):
         regroup1(0)
         w_grouped = keep.tile([P, 2, P, PACK], BF16, align_bytes=64)
         regroup_two_rows(nc.scalar.copy, w_bank, w_grouped[:].bitcast(F32))
-        bias_free = keep.tile([P, FEATURES], F32)
-        nc.scalar.copy(out=bias_free[:], in_=bias_bank[:])
         quantise1(0)
         w_codes = keep.tile([P, 2, P], U32, align_bytes=64)
         w_scales = keep.tile([P, 2, P], U8, align_bytes=64)
@@ -198,6 +212,13 @@ def tile_simplemodel_pc_t_kernel(tc, h1, cross_w, cross_b, out):
             scales=w_scales[:].rearrange("p e q -> p (e q)"),
             in_=w_grouped[:].rearrange("p e q t -> p (e q t)"),
         )
+
+        bias_free = keep.tile([P, FEATURES], F32)
+
+        def spread_bias():
+            bias_bank = psum_2.tile([P, FEATURES], F32, tag="level2")
+            nc.tensor.matmul(out=bias_bank[:], lhsT=ones[:, :P], rhs=bias_row[:], start=True, stop=True)
+            nc.scalar.copy(out=bias_free[:], in_=bias_bank[:])
 
         def run(stage, token):
             if 0 <= token < TOKENS:
@@ -212,4 +233,6 @@ def tile_simplemodel_pc_t_kernel(tc, h1, cross_w, cross_b, out):
             run(regroup2, step - 1)
             run(quantise2, step - 2)
             run(finish, step - 3)
+            if step == 1:
+                spread_bias()
             run(transposes, step + 2)

@@ -19,7 +19,6 @@ K = 2 * FEATURES
 WORDS = K // 2
 ROWS1 = 4
 SHARED_TOKENS = 4
-WARM_MATMULS = 3
 WARM_COLS = 512
 PAIRS = 2
 
@@ -54,6 +53,8 @@ def tile_simplemodel_pc_t_kernel(tc, h1, cross_w, cross_b, out):
         load_pair(1, 1)
         for token in range(2, TOKENS):
             nc.sync.dma_start(out=x_all[:, token], in_=h1_rows[:, token])
+        table_load = keep.tile([P, 1], BF16)
+        nc.scalar.copy(out=table_load[:], in_=ones[:, :1])
         bias_pair = keep.tile([P, 2], BF16)
         nc.scalar.dma_start(out=bias_pair[:], in_=cross_b.rearrange("(q e) -> q e", e=2))
         bias_row = keep.tile([P, FEATURES], BF16)
@@ -105,7 +106,7 @@ def tile_simplemodel_pc_t_kernel(tc, h1, cross_w, cross_b, out):
             codes1[token] = (g1_codes, g1_scales)
 
         def on_scalar(token):
-            return token % 2 == 1
+            return token < TOKENS - 1 and (token % 2 == 1 or token == TOKENS - 2)
 
         def level1(token):
             g1_codes, g1_scales = codes1[token]
@@ -146,6 +147,15 @@ def tile_simplemodel_pc_t_kernel(tc, h1, cross_w, cross_b, out):
                     )
             else:
                 for j in range(PAIRS):
+                    if j == 1 and token == TOKENS - 1:
+                        for e in range(2):
+                            nc.scalar.activation(
+                                out=g2_grouped[:, j, :, :, e],
+                                in_=banks1[token][j][:, e, :].rearrange("q (u b) -> q b u", u=2),
+                                func=IDENTITY,
+                                bias=bias_part[:, e : e + 1],
+                            )
+                        continue
                     nc.vector.tensor_tensor(
                         out=g2_grouped[:, j],
                         in0=banks1[token][j][:].rearrange("q e (u b) -> q b u e", u=2),
@@ -191,16 +201,18 @@ def tile_simplemodel_pc_t_kernel(tc, h1, cross_w, cross_b, out):
                 )
                 nc.sync.dma_start(out=out[:, token, part], in_=out_all[:, token, part])
 
-        warm_bank = psum_2.tile([P, WARM_COLS], F32, tag="level2")
-        for i in range(WARM_MATMULS):
-            nc.tensor.matmul(out=warm_bank[:], lhsT=ones[:, :P], rhs=ones[:], start=True, stop=True)
+        def keep_warm(matmuls):
+            warm_bank = psum_2.tile([P, WARM_COLS], F32, tag="level2")
+            for i in range(matmuls):
+                nc.tensor.matmul(out=warm_bank[:], lhsT=ones[:, :P], rhs=ones[:], start=True, stop=True)
+
+        keep_warm(4)
         transposes(0)
+        keep_warm(2)
         w_bank = psum_1.tile([P, 2, 2, P], F32, tag="level1")
         transpose_two_rows(w_rows[:].bitcast(F32), w_bank)
         transposes(1)
 
-        bias_part = keep.tile([P, 2], F32)
-        nc.vector.tensor_copy(out=bias_part[:], in_=bias_pair[:])
         regroup1(0)
         w_grouped = keep.tile([P, 2, P, PACK], BF16, align_bytes=64)
         regroup_two_rows(nc.scalar.copy, w_bank, w_grouped[:].bitcast(F32))
@@ -212,6 +224,8 @@ def tile_simplemodel_pc_t_kernel(tc, h1, cross_w, cross_b, out):
             scales=w_scales[:].rearrange("p e q -> p (e q)"),
             in_=w_grouped[:].rearrange("p e q t -> p (e q t)"),
         )
+        bias_part = keep.tile([P, 2], F32)
+        nc.vector.tensor_copy(out=bias_part[:], in_=bias_pair[:])
 
         bias_free = keep.tile([P, FEATURES], F32)
 
@@ -235,4 +249,6 @@ def tile_simplemodel_pc_t_kernel(tc, h1, cross_w, cross_b, out):
             run(finish, step - 3)
             if step == 1:
                 spread_bias()
+            if step == 0:
+                keep_warm(2)
             run(transposes, step + 2)

@@ -7,6 +7,7 @@ F32 = mybir.dt.float32
 BF16 = mybir.dt.bfloat16
 U32 = mybir.dt.uint32
 U8 = mybir.dt.uint8
+I32 = mybir.dt.int32
 FP8X4 = mybir.dt.float8_e4m3fn_x4
 ADD = mybir.AluOpType.add
 IDENTITY = mybir.ActivationFunctionType.Identity
@@ -106,7 +107,7 @@ def tile_simplemodel_pc_t_kernel(tc, h1, cross_w, cross_b, out):
             codes1[token] = (g1_codes, g1_scales)
 
         def on_scalar(token):
-            return token < TOKENS - 1 and (token % 2 == 1 or token == TOKENS - 2)
+            return token % 3 != 2
 
         def level1(token):
             g1_codes, g1_scales = codes1[token]
@@ -136,30 +137,25 @@ def tile_simplemodel_pc_t_kernel(tc, h1, cross_w, cross_b, out):
                     banks1[token].append(h2_bank)
 
         def regroup2(token):
-            g2_grouped = ring.tile([P, PAIRS, P, 2, 2], BF16, align_bytes=64)
+            g2_grouped = ring.tile([P, PAIRS * P, PACK], BF16, align_bytes=64)
             if on_scalar(token):
+                planes = ring.tile([P, 2, PAIRS * P * 2], BF16, align_bytes=64)
                 for e in range(2):
                     nc.scalar.activation(
-                        out=g2_grouped[:, :, :, :, e],
+                        out=planes[:, e, :].rearrange("q (j b u) -> q j b u", j=PAIRS, u=2),
                         in_=banks1[token][e][:].rearrange("q (j u b) -> q j b u", j=PAIRS, u=2),
                         func=IDENTITY,
                         bias=bias_part[:, e : e + 1],
                     )
+                nc.gpsimd.tensor_copy(
+                    out=g2_grouped[:].bitcast(I32), in_=planes[:].bitcast(I32).rearrange("q e n -> q n e")
+                )
             else:
                 for j in range(PAIRS):
-                    if j == 1 and token == TOKENS - 1:
-                        for e in range(2):
-                            nc.scalar.activation(
-                                out=g2_grouped[:, j, :, :, e],
-                                in_=banks1[token][j][:, e, :].rearrange("q (u b) -> q b u", u=2),
-                                func=IDENTITY,
-                                bias=bias_part[:, e : e + 1],
-                            )
-                        continue
                     nc.vector.tensor_tensor(
-                        out=g2_grouped[:, j],
-                        in0=banks1[token][j][:].rearrange("q e (u b) -> q b u e", u=2),
-                        in1=bias_part[:].unsqueeze(1).unsqueeze(1).to_broadcast([P, P, 2, 2]),
+                        out=g2_grouped[:, j * P : (j + 1) * P, :].rearrange("q b (e u) -> q b e u", e=2),
+                        in0=banks1[token][j][:].rearrange("q e (u b) -> q b e u", u=2),
+                        in1=bias_part[:].unsqueeze(1).unsqueeze(3).to_broadcast([P, P, 2, 2]),
                         op=ADD,
                     )
             grouped2[token] = g2_grouped
@@ -170,7 +166,7 @@ def tile_simplemodel_pc_t_kernel(tc, h1, cross_w, cross_b, out):
             nc.vector.quantize_mx(
                 out=g2_codes[:].bitcast(FP8X4),
                 scales=g2_scales[:],
-                in_=grouped2[token][:].rearrange("p j b u e -> p (j b u e)"),
+                in_=grouped2[token][:].rearrange("p n t -> p (n t)"),
             )
             codes2[token] = (g2_codes, g2_scales)
 
@@ -182,8 +178,8 @@ def tile_simplemodel_pc_t_kernel(tc, h1, cross_w, cross_b, out):
                     out=out_bank[:, j, :],
                     lhsT=g2_codes[:, j * P : (j + 1) * P].bitcast(FP8X4),
                     lhsT_scale=g2_scales[:, j * P : (j + 1) * P],
-                    rhs=w_codes[:].rearrange("p e q -> p (e q)").bitcast(FP8X4),
-                    rhs_scale=w_scales[:].rearrange("p e q -> p (e q)"),
+                    rhs=w2_codes[:].bitcast(FP8X4),
+                    rhs_scale=w2_scales[:],
                     start=True,
                     stop=True,
                 )
@@ -234,6 +230,23 @@ def tile_simplemodel_pc_t_kernel(tc, h1, cross_w, cross_b, out):
             nc.tensor.matmul(out=bias_bank[:], lhsT=ones[:, :P], rhs=bias_row[:], start=True, stop=True)
             nc.scalar.copy(out=bias_free[:], in_=bias_bank[:])
 
+        w2_grouped = keep.tile([P, 2 * P, PACK], BF16, align_bytes=64)
+        w2_codes = keep.tile([P, 2 * P], U32, align_bytes=64)
+        w2_scales = keep.tile([P, 2 * P], U8, align_bytes=64)
+
+        def reorder_weights():
+            nc.scalar.copy(
+                out=w2_grouped[:].rearrange("p n (e u) -> p n e u", e=2),
+                in_=w_grouped[:].rearrange("p r q (u e) -> p (r q) e u", e=2),
+            )
+
+        def quantise_weights2():
+            nc.vector.quantize_mx(
+                out=w2_codes[:].bitcast(FP8X4),
+                scales=w2_scales[:],
+                in_=w2_grouped[:].rearrange("p n t -> p (n t)"),
+            )
+
         def run(stage, token):
             if 0 <= token < TOKENS:
                 stage(token)
@@ -249,6 +262,9 @@ def tile_simplemodel_pc_t_kernel(tc, h1, cross_w, cross_b, out):
             run(finish, step - 3)
             if step == 1:
                 spread_bias()
+                reorder_weights()
+            if step == 2:
+                quantise_weights2()
             if step == 0:
                 keep_warm(2)
             run(transposes, step + 2)

@@ -19,7 +19,8 @@ FEATURES = 256
 K = 2 * FEATURES
 WORDS = K // 2
 ROWS1 = 4
-SHARED_TOKENS = 4
+SHARED_TOKENS = (0, 3)
+DRAIN = 13
 WARM_COLS = 512
 PAIRS = 2
 
@@ -91,7 +92,7 @@ def tile_simplemodel_pc_t_kernel(tc, h1, cross_w, cross_b, out):
 
         def regroup1(token):
             g1_grouped = ring.tile([P, ROWS1, P, PACK], BF16, align_bytes=64)
-            second = nc.vector.tensor_copy if token < SHARED_TOKENS else nc.scalar.copy
+            second = nc.vector.tensor_copy if token in SHARED_TOKENS else nc.scalar.copy
             for j, copy in enumerate((nc.scalar.copy, second)):
                 regroup_two_rows(copy, t_banks[token][j], g1_grouped[:, 2 * j : 2 * j + 2].bitcast(F32))
             grouped1[token] = g1_grouped
@@ -107,7 +108,7 @@ def tile_simplemodel_pc_t_kernel(tc, h1, cross_w, cross_b, out):
             codes1[token] = (g1_codes, g1_scales)
 
         def on_scalar(token):
-            return token % 3 != 2
+            return token >= DRAIN or token % 5 in (1, 3, 4)
 
         def level1(token):
             g1_codes, g1_scales = codes1[token]
@@ -138,7 +139,15 @@ def tile_simplemodel_pc_t_kernel(tc, h1, cross_w, cross_b, out):
 
         def regroup2(token):
             g2_grouped = ring.tile([P, PAIRS * P, PACK], BF16, align_bytes=64)
-            if on_scalar(token):
+            if token >= DRAIN:
+                for e in range(2):
+                    nc.scalar.activation(
+                        out=g2_grouped[:].rearrange("q (j b) (e u) -> q j b e u", j=PAIRS, e=2)[:, :, :, e, :],
+                        in_=banks1[token][e][:].rearrange("q (j u b) -> q j b u", j=PAIRS, u=2),
+                        func=IDENTITY,
+                        bias=bias_part[:, e : e + 1],
+                    )
+            elif on_scalar(token):
                 planes = ring.tile([P, 2, PAIRS * P * 2], BF16, align_bytes=64)
                 for e in range(2):
                     nc.scalar.activation(
@@ -234,11 +243,10 @@ def tile_simplemodel_pc_t_kernel(tc, h1, cross_w, cross_b, out):
         w2_codes = keep.tile([P, 2 * P], U32, align_bytes=64)
         w2_scales = keep.tile([P, 2 * P], U8, align_bytes=64)
 
-        def reorder_weights():
-            nc.scalar.copy(
-                out=w2_grouped[:].rearrange("p n (e u) -> p n e u", e=2),
-                in_=w_grouped[:].rearrange("p r q (u e) -> p (r q) e u", e=2),
-            )
+        nc.vector.tensor_copy(
+            out=w2_grouped[:].rearrange("p n (e u) -> p n e u", e=2),
+            in_=w_grouped[:].rearrange("p r q (u e) -> p (r q) e u", e=2),
+        )
 
         def quantise_weights2():
             nc.vector.quantize_mx(
@@ -247,6 +255,9 @@ def tile_simplemodel_pc_t_kernel(tc, h1, cross_w, cross_b, out):
                 in_=w2_grouped[:].rearrange("p n t -> p (n t)"),
             )
 
+        def lag(token):
+            return 3 if token < DRAIN else 2
+
         def run(stage, token):
             if 0 <= token < TOKENS:
                 stage(token)
@@ -254,17 +265,21 @@ def tile_simplemodel_pc_t_kernel(tc, h1, cross_w, cross_b, out):
         for step in range(TOKENS + 3):
             if step > 0:
                 run(quantise1, step)
+            if step == 1:
+                quantise_weights2()
             run(level1, step - 1)
-            run(level2, step - 3)
+            ready = [token for token in range(TOKENS) if token + lag(token) + 1 == step]
+            for token in ready:
+                level2(token)
+            for token in range(TOKENS):
+                if token + lag(token) == step:
+                    quantise2(token)
             run(regroup1, step + 1)
             run(regroup2, step - 1)
-            run(quantise2, step - 2)
-            run(finish, step - 3)
+            for token in ready:
+                finish(token)
             if step == 1:
                 spread_bias()
-                reorder_weights()
-            if step == 2:
-                quantise_weights2()
             if step == 0:
                 keep_warm(2)
             run(transposes, step + 2)

@@ -262,22 +262,23 @@ def tile_simplemodel_pc_t_kernel(tc, h1, cross_w, cross_b, out):
             if 0 <= token < TOKENS:
                 stage(token)
 
-        for step in range(TOKENS + 3):
+        for step in range(TOKENS + 4):
             if step > 0:
                 run(quantise1, step)
             if step == 1:
                 quantise_weights2()
             run(level1, step - 1)
-            ready = [token for token in range(TOKENS) if token + lag(token) + 1 == step]
-            for token in ready:
-                level2(token)
+            run(regroup1, step + 1)
+            for token in range(TOKENS):
+                if token + lag(token) + 2 == step:
+                    finish(token)
+            for token in range(TOKENS):
+                if token + lag(token) + 1 == step:
+                    level2(token)
+            run(regroup2, step - 1)
             for token in range(TOKENS):
                 if token + lag(token) == step:
                     quantise2(token)
-            run(regroup1, step + 1)
-            run(regroup2, step - 1)
-            for token in ready:
-                finish(token)
             if step == 1:
                 spread_bias()
             if step == 0:

from contextlib import ExitStack

import concourse.mybir as mybir
from concourse.masks import make_identity

F32 = mybir.dt.float32
BF16 = mybir.dt.bfloat16
U32 = mybir.dt.uint32
U8 = mybir.dt.uint8
I32 = mybir.dt.int32
FP8X4 = mybir.dt.float8_e4m3fn_x4
ADD = mybir.AluOpType.add
IDENTITY = mybir.ActivationFunctionType.Identity

P = 128
PACK = 4
TOKENS = 16
FEATURES = 256
K = 2 * FEATURES
WORDS = K // 2
ROWS1 = 4
SHARED_TOKENS = (0, 3)
DRAIN = 13
WARM_COLS = 512
PAIRS = 2

FLOPS = 2 * P * TOKENS * (ROWS1 + PAIRS) * K * FEATURES


def tile_simplemodel_pc_t_kernel(tc, h1, cross_w, cross_b, out):
    nc = tc.nc
    h1_rows = h1.rearrange("b i (m n) f -> b i m (n f)", n=2)

    with ExitStack() as ctx:
        ctx.enter_context(tc.manual_schedule())
        keep = ctx.enter_context(tc.tile_pool(name="keep", bufs=1))
        ring = ctx.enter_context(tc.tile_pool(name="ring", bufs=3))
        psum_t = ctx.enter_context(tc.psum_pool(name="psum_t", bufs=3))
        psum_1 = ctx.enter_context(tc.psum_pool(name="psum_1", bufs=3))
        psum_2 = ctx.enter_context(tc.psum_pool(name="psum_2", bufs=2))

        ones = keep.tile([P, WARM_COLS], BF16)
        nc.vector.memset(ones[:], 1.0)
        x_all = keep.tile([P, TOKENS, ROWS1, K], BF16)

        def load_pair(token, j):
            rows = slice(2 * j, 2 * j + 2)
            nc.sync.dma_start(out=x_all[:, token, rows], in_=h1_rows[:, token, rows])

        load_pair(0, 0)
        load_pair(0, 1)
        w_rows = keep.tile([P, 2, K], BF16)
        nc.sync.dma_start(out=w_rows[:], in_=cross_w.rearrange("(q e) k -> q e k", e=2))
        load_pair(1, 0)
        load_pair(1, 1)
        for token in range(2, TOKENS):
            nc.sync.dma_start(out=x_all[:, token], in_=h1_rows[:, token])
        table_load = keep.tile([P, 1], BF16)
        nc.scalar.copy(out=table_load[:], in_=ones[:, :1])
        bias_pair = keep.tile([P, 2], BF16)
        nc.scalar.dma_start(out=bias_pair[:], in_=cross_b.rearrange("(q e) -> q e", e=2))
        bias_row = keep.tile([P, FEATURES], BF16)
        nc.vector.memset(bias_row[:], 0.0)
        nc.scalar.dma_start(out=bias_row[0:1, :], in_=cross_b.unsqueeze(0))
        out_all = keep.tile([P, TOKENS, PAIRS, FEATURES], F32)

        ident = keep.tile([P, P], F32)
        make_identity(nc, ident[:])

        def transpose_two_rows(words, bank):
            for r in range(2):
                for u in range(2):
                    nc.tensor.transpose(bank[:, r, u, :], words[:, r, u * P : (u + 1) * P], ident[:])

        def regroup_two_rows(copy, bank, grouped_words):
            copy(out=grouped_words, in_=bank[:].rearrange("q r u c -> q r c u"))

        t_banks = {}
        grouped1 = {}
        codes1 = {}
        banks1 = {}
        grouped2 = {}
        codes2 = {}
        banks2 = {}

        def transposes(token):
            t_banks[token] = []
            for j in range(PAIRS):
                t_bank = psum_t.tile([P, 2, 2, P], F32, tag="transposed")
                transpose_two_rows(x_all[:, token, 2 * j : 2 * j + 2, :].bitcast(F32), t_bank)
                t_banks[token].append(t_bank)

        def regroup1(token):
            g1_grouped = ring.tile([P, ROWS1, P, PACK], BF16, align_bytes=64)
            second = nc.vector.tensor_copy if token in SHARED_TOKENS else nc.scalar.copy
            for j, copy in enumerate((nc.scalar.copy, second)):
                regroup_two_rows(copy, t_banks[token][j], g1_grouped[:, 2 * j : 2 * j + 2].bitcast(F32))
            grouped1[token] = g1_grouped

        def quantise1(token):
            g1_codes = ring.tile([P, ROWS1 * P], U32, align_bytes=64)
            g1_scales = ring.tile([P, ROWS1 * P], U8, align_bytes=64)
            nc.vector.quantize_mx(
                out=g1_codes[:].bitcast(FP8X4),
                scales=g1_scales[:],
                in_=grouped1[token][:].rearrange("p m b t -> p (m b t)"),
            )
            codes1[token] = (g1_codes, g1_scales)

        def on_scalar(token):
            return token >= DRAIN or token % 5 in (1, 3, 4)

        def level1(token):
            g1_codes, g1_scales = codes1[token]
            banks1[token] = []

            def one_pass(product, e, cols):
                nc.tensor.matmul_mx(
                    out=product,
                    lhsT=w_codes[:, e, :].bitcast(FP8X4),
                    lhsT_scale=w_scales[:, e, :],
                    rhs=g1_codes[:, cols].bitcast(FP8X4),
                    rhs_scale=g1_scales[:, cols],
                    start=True,
                    stop=True,
                )

            if on_scalar(token):
                for e in range(2):
                    h2_bank = psum_1.tile([P, ROWS1 * P], F32, tag="level1")
                    one_pass(h2_bank[:], e, slice(0, ROWS1 * P))
                    banks1[token].append(h2_bank)
            else:
                for j in range(PAIRS):
                    h2_bank = psum_1.tile([P, 2, 2 * P], F32, tag="level1")
                    for e in range(2):
                        one_pass(h2_bank[:, e, :], e, slice(j * 2 * P, (j + 1) * 2 * P))
                    banks1[token].append(h2_bank)

        def regroup2(token):
            g2_grouped = ring.tile([P, PAIRS * P, PACK], BF16, align_bytes=64)
            if token >= DRAIN:
                for e in range(2):
                    nc.scalar.activation(
                        out=g2_grouped[:].rearrange("q (j b) (e u) -> q j b e u", j=PAIRS, e=2)[:, :, :, e, :],
                        in_=banks1[token][e][:].rearrange("q (j u b) -> q j b u", j=PAIRS, u=2),
                        func=IDENTITY,
                        bias=bias_part[:, e : e + 1],
                    )
            elif on_scalar(token):
                planes = ring.tile([P, 2, PAIRS * P * 2], BF16, align_bytes=64)
                for e in range(2):
                    nc.scalar.activation(
                        out=planes[:, e, :].rearrange("q (j b u) -> q j b u", j=PAIRS, u=2),
                        in_=banks1[token][e][:].rearrange("q (j u b) -> q j b u", j=PAIRS, u=2),
                        func=IDENTITY,
                        bias=bias_part[:, e : e + 1],
                    )
                nc.gpsimd.tensor_copy(
                    out=g2_grouped[:].bitcast(I32), in_=planes[:].bitcast(I32).rearrange("q e n -> q n e")
                )
            else:
                for j in range(PAIRS):
                    nc.vector.tensor_tensor(
                        out=g2_grouped[:, j * P : (j + 1) * P, :].rearrange("q b (e u) -> q b e u", e=2),
                        in0=banks1[token][j][:].rearrange("q e (u b) -> q b e u", u=2),
                        in1=bias_part[:].unsqueeze(1).unsqueeze(3).to_broadcast([P, P, 2, 2]),
                        op=ADD,
                    )
            grouped2[token] = g2_grouped

        def quantise2(token):
            g2_codes = ring.tile([P, PAIRS * P], U32, align_bytes=64)
            g2_scales = ring.tile([P, PAIRS * P], U8, align_bytes=64)
            nc.vector.quantize_mx(
                out=g2_codes[:].bitcast(FP8X4),
                scales=g2_scales[:],
                in_=grouped2[token][:].rearrange("p n t -> p (n t)"),
            )
            codes2[token] = (g2_codes, g2_scales)

        def level2(token):
            g2_codes, g2_scales = codes2[token]
            out_bank = psum_2.tile([P, PAIRS, FEATURES], F32, tag="level2")
            for j in range(PAIRS):
                nc.tensor.matmul_mx(
                    out=out_bank[:, j, :],
                    lhsT=g2_codes[:, j * P : (j + 1) * P].bitcast(FP8X4),
                    lhsT_scale=g2_scales[:, j * P : (j + 1) * P],
                    rhs=w2_codes[:].bitcast(FP8X4),
                    rhs_scale=w2_scales[:],
                    start=True,
                    stop=True,
                )
            banks2[token] = out_bank

        def finish(token):
            parts = [slice(0, PAIRS)] if token < TOKENS - 1 else [slice(j, j + 1) for j in range(PAIRS)]
            for part in parts:
                pairs = part.stop - part.start
                nc.vector.tensor_tensor(
                    out=out_all[:, token, part].rearrange("b j (q e) -> b j q e", e=2),
                    in0=banks2[token][:, part].rearrange("b j (e q) -> b j q e", e=2),
                    in1=bias_free[:].rearrange("b (q e) -> b q e", e=2).unsqueeze(1).to_broadcast([P, pairs, P, 2]),
                    op=ADD,
                )
                nc.sync.dma_start(out=out[:, token, part], in_=out_all[:, token, part])

        def keep_warm(matmuls):
            warm_bank = psum_2.tile([P, WARM_COLS], F32, tag="level2")
            for i in range(matmuls):
                nc.tensor.matmul(out=warm_bank[:], lhsT=ones[:, :P], rhs=ones[:], start=True, stop=True)

        keep_warm(4)
        transposes(0)
        keep_warm(2)
        w_bank = psum_1.tile([P, 2, 2, P], F32, tag="level1")
        transpose_two_rows(w_rows[:].bitcast(F32), w_bank)
        transposes(1)

        regroup1(0)
        w_grouped = keep.tile([P, 2, P, PACK], BF16, align_bytes=64)
        regroup_two_rows(nc.scalar.copy, w_bank, w_grouped[:].bitcast(F32))
        quantise1(0)
        w_codes = keep.tile([P, 2, P], U32, align_bytes=64)
        w_scales = keep.tile([P, 2, P], U8, align_bytes=64)
        nc.vector.quantize_mx(
            out=w_codes[:].rearrange("p e q -> p (e q)").bitcast(FP8X4),
            scales=w_scales[:].rearrange("p e q -> p (e q)"),
            in_=w_grouped[:].rearrange("p e q t -> p (e q t)"),
        )
        bias_part = keep.tile([P, 2], F32)
        nc.vector.tensor_copy(out=bias_part[:], in_=bias_pair[:])

        bias_free = keep.tile([P, FEATURES], F32)

        def spread_bias():
            bias_bank = psum_2.tile([P, FEATURES], F32, tag="level2")
            nc.tensor.matmul(out=bias_bank[:], lhsT=ones[:, :P], rhs=bias_row[:], start=True, stop=True)
            nc.scalar.copy(out=bias_free[:], in_=bias_bank[:])

        w2_grouped = keep.tile([P, 2 * P, PACK], BF16, align_bytes=64)
        w2_codes = keep.tile([P, 2 * P], U32, align_bytes=64)
        w2_scales = keep.tile([P, 2 * P], U8, align_bytes=64)

        nc.vector.tensor_copy(
            out=w2_grouped[:].rearrange("p n (e u) -> p n e u", e=2),
            in_=w_grouped[:].rearrange("p r q (u e) -> p (r q) e u", e=2),
        )

        def quantise_weights2():
            nc.vector.quantize_mx(
                out=w2_codes[:].bitcast(FP8X4),
                scales=w2_scales[:],
                in_=w2_grouped[:].rearrange("p n t -> p (n t)"),
            )

        def lag(token):
            return 3 if token < DRAIN else 2

        def run(stage, token):
            if 0 <= token < TOKENS:
                stage(token)

        for step in range(TOKENS + 4):
            if step > 0:
                run(quantise1, step)
            if step == 1:
                quantise_weights2()
            run(level1, step - 1)
            run(regroup1, step + 1)
            for token in range(TOKENS):
                if token + lag(token) + 2 == step:
                    finish(token)
            for token in range(TOKENS):
                if token + lag(token) + 1 == step:
                    level2(token)
            run(regroup2, step - 1)
            for token in range(TOKENS):
                if token + lag(token) == step:
                    quantise2(token)
            if step == 1:
                spread_bias()
            if step == 0:
                keep_warm(2)
            run(transposes, step + 2)
